import numpy as np
import ml_dtypes


def mxq(x, axis, fmt="e4m3"):
    dtype, down = {"e4m3": (ml_dtypes.float8_e4m3fn, 7), "e5m2": (ml_dtypes.float8_e5m2, 14)}[fmt]
    v = np.moveaxis(np.asarray(x, np.float32).astype(ml_dtypes.bfloat16).astype(np.float64), axis, -1)
    blocks = v.reshape(v.shape[:-1] + (-1, 32))
    amax = np.abs(blocks).max(-1, keepdims=True)
    byte = np.maximum(np.where(amax > 0, np.frexp(amax)[1] - 1 + 127, 0) - down, 1)
    scale = np.exp2(byte - 127.0)
    codes = (blocks / scale).astype(np.float32).astype(dtype).astype(np.float64)
    return np.moveaxis((codes * scale).reshape(v.shape), -1, axis)


BF16 = ml_dtypes.bfloat16


def bf(x):
    return np.asarray(x, np.float32).astype(BF16)


def f64(x):
    return np.asarray(x).astype(np.float64)


B, C, H, W, N, K, R = 2, 512, 32, 32, 4, 32, 8

ENSEMBLE_MAX_MEAN = 0.5
EPS = 1e-12


def _l2norm(x, axis):
    return x / np.sqrt(np.sum(x * x, axis=axis, keepdims=True) + EPS)


def setup_inputs():
    g = np.random.standard_normal((R, C)) / np.sqrt(R)
    x = np.random.standard_normal((B, C, H, W))
    p = np.random.standard_normal((N, K, C))
    for r in range(R):
        x += np.random.standard_normal((B, 1, H, W)) * g[r][None, :, None, None]
        p += (np.random.standard_normal((N, 1, 1)) + np.random.standard_normal((N, K, 1))) * np.sqrt(0.5) * g[r]
    return {"image_feat": bf(x), "proto_emb": bf(p)}


def reference(image_feat, proto_emb):
    img = _l2norm(f64(image_feat), 1)
    pro = _l2norm(f64(proto_emb), -1)
    imgq = mxq(img, 1, "e4m3").reshape(B, C, H * W)
    proq = mxq(pro, 2, "e4m3").reshape(N * K, C)
    simmap = (proq @ imgq).reshape(B, N, K, H, W)
    sim_max = np.max(simmap, axis=2)
    sim_mean = np.mean(simmap, axis=2)
    sim = ENSEMBLE_MAX_MEAN * sim_max + (1.0 - ENSEMBLE_MAX_MEAN) * sim_mean
    soft_mask = 1.0 / (1.0 + np.exp(-sim))
    return soft_mask, sim

@@ -1,0 +1,183 @@
+from contextlib import ExitStack
+
+import concourse.mybir as mybir
+from concourse.masks import make_identity
+
+BF16 = mybir.dt.bfloat16
+F32 = mybir.dt.float32
+U32 = mybir.dt.uint32
+U8 = mybir.dt.uint8
+FP8X4 = mybir.dt.float8_e4m3fn_x4
+ACT = mybir.ActivationFunctionType
+ALU = mybir.AluOpType
+AXIS_X = mybir.AxisListType.X
+
+P = 128
+PACK = 4
+BATCH = 2
+CHANNELS = P * PACK
+PIXELS = 1024
+CLASSES = 4
+PER_CLASS = 32
+PROTOS = CLASSES * PER_CLASS
+TILES_PER_IMAGE = PIXELS // P
+CHUNK_TILES = 2
+CHUNK = CHUNK_TILES * P
+EPS = 1e-12
+
+FLOPS = 2 * PROTOS * CHANNELS * BATCH * PIXELS
+
+
+def tile_freedamasker_s_kernel(tc, image_feat, proto_emb, out_0, out_1):
+    nc = tc.nc
+    with ExitStack() as ctx:
+        const = ctx.enter_context(tc.tile_pool(name="const", bufs=1))
+        keep = ctx.enter_context(tc.tile_pool(name="keep", bufs=1))
+        junk_pool = ctx.enter_context(tc.tile_pool(name="junk", bufs=4))
+        small = ctx.enter_context(tc.tile_pool(name="small", bufs=4))
+        work = ctx.enter_context(tc.tile_pool(name="work", bufs=3))
+        ps_xt = ctx.enter_context(tc.psum_pool(name="ps_xt", bufs=3))
+        ps_bc = ctx.enter_context(tc.psum_pool(name="ps_bc", bufs=2))
+        ps_sim = ctx.enter_context(tc.psum_pool(name="ps_sim", bufs=2))
+        ps_misc = ctx.enter_context(tc.psum_pool(name="ps_misc", bufs=1))
+
+        pro_raw = keep.tile([P, CHANNELS], BF16)
+        nc.scalar.dma_start(out=pro_raw[:], in_=proto_emb.rearrange("n k c -> (n k) c"))
+        chunks = [(b, w0) for b in range(BATCH) for w0 in range(0, PIXELS, CHUNK)]
+        x_tiles = []
+        for b, w0 in chunks:
+            x_sb = keep.tile([P, PACK, CHUNK], BF16, name="x_%d_%d" % (b, w0))
+            src = image_feat[b].rearrange("(p j) h w -> p j (h w)", j=PACK)
+            nc.sync.dma_start(out=x_sb[:], in_=src[:, :, w0 : w0 + CHUNK])
+            x_tiles.append(x_sb)
+
+        ident_bf = const.tile([P, P], BF16)
+        make_identity(nc, ident_bf[:])
+        ident_f32 = const.tile([P, P], F32)
+        make_identity(nc, ident_f32[:])
+        one = const.tile([P, 1], F32)
+        nc.vector.memset(one[:], 1.0)
+        warm = const.tile([P, 1], F32)
+        nc.scalar.activation(out=warm[:], in_=one[:], func=ACT.Sqrt)
+
+        pro_ss = small.tile([P, 1], F32)
+        pro_junk = junk_pool.tile([P, CHANNELS], BF16, tag="junk")
+        nc.scalar.activation(out=pro_junk[:], in_=pro_raw[:], func=ACT.Square, accum_out=pro_ss[:])
+        pro_norm = small.tile([P, 1], F32)
+        nc.scalar.activation(out=pro_norm[:], in_=pro_ss[:], func=ACT.Sqrt, bias=EPS)
+        pro_rn = small.tile([P, 1], F32)
+        nc.vector.reciprocal(out=pro_rn[:], in_=pro_norm[:])
+        pro_unit = keep.tile([P, PACK, P], BF16)
+        nc.vector.tensor_scalar(
+            out=pro_unit[:],
+            in0=pro_raw[:].rearrange("m (p t) -> m t p", t=PACK),
+            scalar1=pro_rn[:, 0:1],
+            scalar2=None,
+            op0=ALU.mult,
+        )
+        pro_t = ps_misc.tile([P, PACK, P], BF16, tag="misc")
+        for t in range(PACK):
+            nc.tensor.transpose(pro_t[:, t, :], pro_unit[:, t, :], ident_bf[:])
+        pro_grouped = keep.tile([P, P, PACK], BF16, align_bytes=64)
+        nc.vector.tensor_copy(out=pro_grouped[:], in_=pro_t[:].rearrange("p t m -> p m t"))
+        pro_codes = keep.tile([P, PROTOS], U32, align_bytes=64)
+        pro_scales = keep.tile([P, PROTOS], U8, align_bytes=64)
+        nc.vector.quantize_mx(
+            out=pro_codes[:].bitcast(FP8X4),
+            scales=pro_scales[:],
+            in_=pro_grouped[:].rearrange("p m t -> p (m t)"),
+        )
+
+        best = keep.tile([P, BATCH, CLASSES, TILES_PER_IMAGE], F32)
+        total = keep.tile([P, BATCH, CLASSES, TILES_PER_IMAGE], F32)
+        last_norm = None
+        for (b, w0), x_sb in zip(chunks, x_tiles):
+            ss = small.tile([P, CHUNK_TILES], F32)
+            for i in range(CHUNK_TILES):
+                xt = ps_xt.tile([P, PACK, P], BF16)
+                for j in range(PACK):
+                    nc.tensor.transpose(xt[:, j, :], x_sb[:, j, i * P : (i + 1) * P], ident_bf[:])
+                junk = junk_pool.tile([P, CHANNELS], BF16, tag="junk")
+                nc.scalar.activation(
+                    out=junk[:],
+                    in_=xt[:].rearrange("m j p -> m (j p)"),
+                    func=ACT.Square,
+                    accum_out=ss[:, i : i + 1],
+                )
+            norm = small.tile([P, CHUNK_TILES], F32)
+            nc.scalar.activation(out=norm[:], in_=ss[:], func=ACT.Sqrt, bias=EPS)
+            last_norm = norm
+            rn = small.tile([P, CHUNK_TILES], F32)
+            nc.vector.reciprocal(out=rn[:], in_=norm[:])
+            bc = ps_bc.tile([P, CHUNK], F32)
+            for i in range(CHUNK_TILES):
+                nc.tensor.transpose(
+                    bc[:, i * P : (i + 1) * P], rn[:, i : i + 1].to_broadcast([P, P]), ident_f32[:]
+                )
+            grouped = work.tile([P, CHUNK, PACK], BF16, align_bytes=64)
+            nc.vector.tensor_tensor(
+                out=grouped[:],
+                in0=x_sb[:].rearrange("p j w -> p w j"),
+                in1=bc[:].unsqueeze(2).to_broadcast([P, CHUNK, PACK]),
+                op=ALU.mult,
+            )
+            codes = work.tile([P, CHUNK], U32, align_bytes=64)
+            scales = work.tile([P, CHUNK], U8, align_bytes=64)
+            nc.vector.quantize_mx(
+                out=codes[:].bitcast(FP8X4),
+                scales=scales[:],
+                in_=grouped[:].rearrange("p w j -> p (w j)"),
+            )
+            sim = ps_sim.tile([P, CHUNK_TILES, PROTOS], F32)
+            for i in range(CHUNK_TILES):
+                cols = slice(i * P, (i + 1) * P)
+                nc.tensor.matmul_mx(
+                    out=sim[:, i, :],
+                    lhsT=codes[:, cols].bitcast(FP8X4),
+                    lhsT_scale=scales[:, cols],
+                    rhs=pro_codes[:].bitcast(FP8X4),
+                    rhs_scale=pro_scales[:],
+                    start=True,
+                    stop=True,
+                )
+            t0 = w0 // P
+            by_class = sim[:].rearrange("m i (n k) -> m i n k", k=PER_CLASS)
+            nc.vector.tensor_reduce(
+                out=best[:, b, :, t0 : t0 + CHUNK_TILES].rearrange("m n i -> m i n"),
+                in_=by_class,
+                axis=AXIS_X,
+                op=ALU.max,
+            )
+            nc.vector.tensor_reduce(
+                out=total[:, b, :, t0 : t0 + CHUNK_TILES].rearrange("m n i -> m i n"),
+                in_=by_class,
+                axis=AXIS_X,
+                op=ALU.add,
+            )
+
+        warm2 = const.tile([P, 1], F32)
+        nc.scalar.activation(out=warm2[:], in_=last_norm[:, 0:1], func=ACT.Sigmoid)
+
+        half = BATCH * CLASSES * TILES_PER_IMAGE
+        both = keep.tile([P, 2, half], F32)
+        nc.vector.scalar_tensor_tensor(
+            out=both[:],
+            in0=total[:].rearrange("m b n t -> m (b n t)").unsqueeze(1).to_broadcast([P, 2, half]),
+            scalar=1.0 / PER_CLASS,
+            in1=best[:].rearrange("m b n t -> m (b n t)").unsqueeze(1).to_broadcast([P, 2, half]),
+            op0=ALU.mult,
+            op1=ALU.add,
+        )
+        both_t = ps_misc.tile([P, P], F32, tag="misc")
+        nc.tensor.transpose(both_t[:], both[:].rearrange("m o c -> m (o c)"), ident_f32[:])
+        result = keep.tile([P, P], F32)
+        nc.vector.tensor_scalar(
+            out=result[0:half, :], in0=both_t[0:half, :], scalar1=0.5, scalar2=None, op0=ALU.mult
+        )
+        nc.scalar.activation(out=result[half:P, :], in_=both_t[half:P, :], func=ACT.Sigmoid, scale=0.5)
+        nc.sync.dma_start(
+            out=out_1.rearrange("b n (t r) w -> (b n t) (r w)", t=TILES_PER_IMAGE), in_=result[0:half, :]
+        )
+        nc.scalar.dma_start(
+            out=out_0.rearrange("b n (t r) w -> (b n t) (r w)", t=TILES_PER_IMAGE), in_=result[half:P, :]
+        )

@@ -31,6 +31,7 @@ FLOPS = 2 * PROTOS * CHANNELS * BATCH * PIXELS
 def tile_freedamasker_s_kernel(tc, image_feat, proto_emb, out_0, out_1):
     nc = tc.nc
     with ExitStack() as ctx:
+        ctx.enter_context(tc.manual_schedule())
         const = ctx.enter_context(tc.tile_pool(name="const", bufs=1))
         keep = ctx.enter_context(tc.tile_pool(name="keep", bufs=1))
         junk_pool = ctx.enter_context(tc.tile_pool(name="junk", bufs=4))
@@ -44,12 +45,13 @@ def tile_freedamasker_s_kernel(tc, image_feat, proto_emb, out_0, out_1):
         pro_raw = keep.tile([P, CHANNELS], BF16)
         nc.scalar.dma_start(out=pro_raw[:], in_=proto_emb.rearrange("n k c -> (n k) c"))
         chunks = [(b, w0) for b in range(BATCH) for w0 in range(0, PIXELS, CHUNK)]
-        x_tiles = []
+        n_chunks = len(chunks)
+        x_of = []
         for b, w0 in chunks:
             x_sb = keep.tile([P, PACK, CHUNK], BF16, name="x_%d_%d" % (b, w0))
             src = image_feat[b].rearrange("(p j) h w -> p j (h w)", j=PACK)
             nc.sync.dma_start(out=x_sb[:], in_=src[:, :, w0 : w0 + CHUNK])
-            x_tiles.append(x_sb)
+            x_of.append(x_sb)
 
         ident_bf = const.tile([P, P], BF16)
         make_identity(nc, ident_bf[:])
@@ -58,45 +60,21 @@ def tile_freedamasker_s_kernel(tc, image_feat, proto_emb, out_0, out_1):
         one = const.tile([P, 1], F32)
         nc.vector.memset(one[:], 1.0)
         warm = const.tile([P, 1], F32)
-        nc.scalar.activation(out=warm[:], in_=one[:], func=ACT.Sqrt)
-
-        pro_ss = small.tile([P, 1], F32)
-        pro_junk = junk_pool.tile([P, CHANNELS], BF16, tag="junk")
-        nc.scalar.activation(out=pro_junk[:], in_=pro_raw[:], func=ACT.Square, accum_out=pro_ss[:])
-        pro_norm = small.tile([P, 1], F32)
-        nc.scalar.activation(out=pro_norm[:], in_=pro_ss[:], func=ACT.Sqrt, bias=EPS)
-        pro_rn = small.tile([P, 1], F32)
-        nc.vector.reciprocal(out=pro_rn[:], in_=pro_norm[:])
-        pro_unit = keep.tile([P, PACK, P], BF16)
-        nc.vector.tensor_scalar(
-            out=pro_unit[:],
-            in0=pro_raw[:].rearrange("m (p t) -> m t p", t=PACK),
-            scalar1=pro_rn[:, 0:1],
-            scalar2=None,
-            op0=ALU.mult,
-        )
-        pro_t = ps_misc.tile([P, PACK, P], BF16, tag="misc")
-        for t in range(PACK):
-            nc.tensor.transpose(pro_t[:, t, :], pro_unit[:, t, :], ident_bf[:])
-        pro_grouped = keep.tile([P, P, PACK], BF16, align_bytes=64)
-        nc.vector.tensor_copy(out=pro_grouped[:], in_=pro_t[:].rearrange("p t m -> p m t"))
-        pro_codes = keep.tile([P, PROTOS], U32, align_bytes=64)
-        pro_scales = keep.tile([P, PROTOS], U8, align_bytes=64)
-        nc.vector.quantize_mx(
-            out=pro_codes[:].bitcast(FP8X4),
-            scales=pro_scales[:],
-            in_=pro_grouped[:].rearrange("p m t -> p (m t)"),
-        )
+        nc.scalar.activation(out=warm[:], in_=one[:], func=ACT.Abs_reciprocal_sqrt)
 
         best = keep.tile([P, BATCH, CLASSES, TILES_PER_IMAGE], F32)
         total = keep.tile([P, BATCH, CLASSES, TILES_PER_IMAGE], F32)
-        last_norm = None
-        for (b, w0), x_sb in zip(chunks, x_tiles):
+        rn_of = {}
+        bc_of = {}
+        grouped_of = {}
+        sim_of = {}
+
+        def pixel_norms(c):
             ss = small.tile([P, CHUNK_TILES], F32)
             for i in range(CHUNK_TILES):
                 xt = ps_xt.tile([P, PACK, P], BF16)
                 for j in range(PACK):
-                    nc.tensor.transpose(xt[:, j, :], x_sb[:, j, i * P : (i + 1) * P], ident_bf[:])
+                    nc.tensor.transpose(xt[:, j, :], x_of[c][:, j, i * P : (i + 1) * P], ident_bf[:])
                 junk = junk_pool.tile([P, CHANNELS], BF16, tag="junk")
                 nc.scalar.activation(
                     out=junk[:],
@@ -104,29 +82,35 @@ def tile_freedamasker_s_kernel(tc, image_feat, proto_emb, out_0, out_1):
                     func=ACT.Square,
                     accum_out=ss[:, i : i + 1],
                 )
-            norm = small.tile([P, CHUNK_TILES], F32)
-            nc.scalar.activation(out=norm[:], in_=ss[:], func=ACT.Sqrt, bias=EPS)
-            last_norm = norm
             rn = small.tile([P, CHUNK_TILES], F32)
-            nc.vector.reciprocal(out=rn[:], in_=norm[:])
+            nc.scalar.activation(out=rn[:], in_=ss[:], func=ACT.Abs_reciprocal_sqrt, bias=EPS)
+            rn_of[c] = rn
+
+        def spread(c):
             bc = ps_bc.tile([P, CHUNK], F32)
             for i in range(CHUNK_TILES):
                 nc.tensor.transpose(
-                    bc[:, i * P : (i + 1) * P], rn[:, i : i + 1].to_broadcast([P, P]), ident_f32[:]
+                    bc[:, i * P : (i + 1) * P], rn_of[c][:, i : i + 1].to_broadcast([P, P]), ident_f32[:]
                 )
+            bc_of[c] = bc
+
+        def normalise(c):
             grouped = work.tile([P, CHUNK, PACK], BF16, align_bytes=64)
             nc.vector.tensor_tensor(
                 out=grouped[:],
-                in0=x_sb[:].rearrange("p j w -> p w j"),
-                in1=bc[:].unsqueeze(2).to_broadcast([P, CHUNK, PACK]),
+                in0=x_of[c][:].rearrange("p j w -> p w j"),
+                in1=bc_of[c][:].unsqueeze(2).to_broadcast([P, CHUNK, PACK]),
                 op=ALU.mult,
             )
+            grouped_of[c] = grouped
+
+        def quantise_and_multiply(c):
             codes = work.tile([P, CHUNK], U32, align_bytes=64)
             scales = work.tile([P, CHUNK], U8, align_bytes=64)
             nc.vector.quantize_mx(
                 out=codes[:].bitcast(FP8X4),
                 scales=scales[:],
-                in_=grouped[:].rearrange("p w j -> p (w j)"),
+                in_=grouped_of[c][:].rearrange("p w j -> p (w j)"),
             )
             sim = ps_sim.tile([P, CHUNK_TILES, PROTOS], F32)
             for i in range(CHUNK_TILES):
@@ -140,23 +124,66 @@ def tile_freedamasker_s_kernel(tc, image_feat, proto_emb, out_0, out_1):
                     start=True,
                     stop=True,
                 )
+            sim_of[c] = sim
+
+        def reduce_over_prototypes(c, op, into):
+            b, w0 = chunks[c]
             t0 = w0 // P
-            by_class = sim[:].rearrange("m i (n k) -> m i n k", k=PER_CLASS)
             nc.vector.tensor_reduce(
-                out=best[:, b, :, t0 : t0 + CHUNK_TILES].rearrange("m n i -> m i n"),
-                in_=by_class,
+                out=into[:, b, :, t0 : t0 + CHUNK_TILES].rearrange("m n i -> m i n"),
+                in_=sim_of[c][:].rearrange("m i (n k) -> m i n k", k=PER_CLASS),
                 axis=AXIS_X,
-                op=ALU.max,
-            )
-            nc.vector.tensor_reduce(
-                out=total[:, b, :, t0 : t0 + CHUNK_TILES].rearrange("m n i -> m i n"),
-                in_=by_class,
-                axis=AXIS_X,
-                op=ALU.add,
+                op=op,
             )
 
+        pro_ss = small.tile([P, 1], F32)
+        pro_junk = junk_pool.tile([P, CHANNELS], BF16, tag="junk")
+        nc.scalar.activation(out=pro_junk[:], in_=pro_raw[:], func=ACT.Square, accum_out=pro_ss[:])
+        pro_rn = small.tile([P, 1], F32)
+        nc.scalar.activation(out=pro_rn[:], in_=pro_ss[:], func=ACT.Abs_reciprocal_sqrt, bias=EPS)
+        pro_unit = keep.tile([P, PACK, P], BF16)
+        nc.vector.tensor_scalar(
+            out=pro_unit[:],
+            in0=pro_raw[:].rearrange("m (p t) -> m t p", t=PACK),
+            scalar1=pro_rn[:, 0:1],
+            scalar2=None,
+            op0=ALU.mult,
+        )
+
+        pixel_norms(0)
+        pixel_norms(1)
+        pro_t = ps_misc.tile([P, PACK, P], BF16, tag="misc")
+        for t in range(PACK):
+            nc.tensor.transpose(pro_t[:, t, :], pro_unit[:, t, :], ident_bf[:])
+        spread(0)
+
+        pro_grouped = keep.tile([P, P, PACK], BF16, align_bytes=64)
+        pro_codes = keep.tile([P, PROTOS], U32, align_bytes=64)
+        pro_scales = keep.tile([P, PROTOS], U8, align_bytes=64)
+
+        for r in range(n_chunks):
+            if r + 2 < n_chunks:
+                pixel_norms(r + 2)
+            normalise(r)
+            if r + 1 < n_chunks:
+                spread(r + 1)
+            if r == 0:
+                nc.vector.tensor_copy(out=pro_grouped[:], in_=pro_t[:].rearrange("p t m -> p m t"))
+                nc.vector.quantize_mx(
+                    out=pro_codes[:].bitcast(FP8X4),
+                    scales=pro_scales[:],
+                    in_=pro_grouped[:].rearrange("p m t -> p (m t)"),
+                )
+            else:
+                reduce_over_prototypes(r - 1, ALU.max, best)
+            quantise_and_multiply(r)
+            if r > 0:
+                reduce_over_prototypes(r - 1, ALU.add, total)
+        reduce_over_prototypes(n_chunks - 1, ALU.max, best)
+        reduce_over_prototypes(n_chunks - 1, ALU.add, total)
+
         warm2 = const.tile([P, 1], F32)
-        nc.scalar.activation(out=warm2[:], in_=last_norm[:, 0:1], func=ACT.Sigmoid)
+        nc.scalar.activation(out=warm2[:], in_=rn_of[n_chunks - 1][:, 0:1], func=ACT.Sigmoid)
 
         half = BATCH * CLASSES * TILES_PER_IMAGE
         both = keep.tile([P, 2, half], F32)

@@ -70,36 +70,33 @@ def tile_freedamasker_s_kernel(tc, image_feat, proto_emb, out_0, out_1):
         sim_of = {}
 
         def pixel_norms(c):
-            ss = small.tile([P, CHUNK_TILES], F32)
-            for i in range(CHUNK_TILES):
-                xt = ps_xt.tile([P, PACK, P], BF16)
-                for j in range(PACK):
-                    nc.tensor.transpose(xt[:, j, :], x_of[c][:, j, i * P : (i + 1) * P], ident_bf[:])
-                junk = junk_pool.tile([P, CHANNELS], BF16, tag="junk")
+            ss = small.tile([P, 2], F32)
+            xt = ps_xt.tile([P, PACK, P], F32)
+            words = x_of[c][:].bitcast(F32)
+            for j in range(PACK):
+                nc.tensor.transpose(xt[:, j, :], words[:, j, :], ident_f32[:])
+            halves = xt[:].bitcast(BF16).rearrange("m j (p e) -> m e j p", e=2)
+            for e in range(2):
+                junk = junk_pool.tile([P, PACK, P], BF16, tag="junk")
                 nc.scalar.activation(
-                    out=junk[:],
-                    in_=xt[:].rearrange("m j p -> m (j p)"),
-                    func=ACT.Square,
-                    accum_out=ss[:, i : i + 1],
+                    out=junk[:], in_=halves[:, e, :, :], func=ACT.Square, accum_out=ss[:, e : e + 1]
                 )
             rn = small.tile([P, CHUNK_TILES], F32)
             nc.scalar.activation(out=rn[:], in_=ss[:], func=ACT.Abs_reciprocal_sqrt, bias=EPS)
             rn_of[c] = rn
 
         def spread(c):
-            bc = ps_bc.tile([P, CHUNK], F32)
-            for i in range(CHUNK_TILES):
-                nc.tensor.transpose(
-                    bc[:, i * P : (i + 1) * P], rn_of[c][:, i : i + 1].to_broadcast([P, P]), ident_f32[:]
-                )
+            bc = ps_bc.tile([P, 2, P], F32)
+            for e in range(2):
+                nc.tensor.transpose(bc[:, e, :], rn_of[c][:, e : e + 1].to_broadcast([P, P]), ident_f32[:])
             bc_of[c] = bc
 
         def normalise(c):
             grouped = work.tile([P, CHUNK, PACK], BF16, align_bytes=64)
             nc.vector.tensor_tensor(
-                out=grouped[:],
-                in0=x_of[c][:].rearrange("p j w -> p w j"),
-                in1=bc_of[c][:].unsqueeze(2).to_broadcast([P, CHUNK, PACK]),
+                out=grouped[:].rearrange("p (m e) j -> p m e j", e=2),
+                in0=x_of[c][:].rearrange("p j (m e) -> p m e j", e=2),
+                in1=bc_of[c][:].rearrange("p e m -> p m e").unsqueeze(3).to_broadcast([P, P, 2, PACK]),
                 op=ALU.mult,
             )
             grouped_of[c] = grouped

@@ -23,6 +23,8 @@ PROTOS = CLASSES * PER_CLASS
 TILES_PER_IMAGE = PIXELS // P
 CHUNK_TILES = 2
 CHUNK = CHUNK_TILES * P
+GPSIMD_PIXELS = 64
+VECTOR_PIXELS = CHUNK - GPSIMD_PIXELS
 EPS = 1e-12
 
 FLOPS = 2 * PROTOS * CHANNELS * BATCH * PIXELS
@@ -64,42 +66,59 @@ def tile_freedamasker_s_kernel(tc, image_feat, proto_emb, out_0, out_1):
 
         best = keep.tile([P, BATCH, CLASSES, TILES_PER_IMAGE], F32)
         total = keep.tile([P, BATCH, CLASSES, TILES_PER_IMAGE], F32)
+        xt_of = {}
         rn_of = {}
         bc_of = {}
         grouped_of = {}
         sim_of = {}
 
+        def transpose_pixels(c):
+            xt_of[c] = []
+            for i in range(CHUNK_TILES):
+                xt = ps_xt.tile([P, PACK, P], BF16)
+                for j in range(PACK):
+                    nc.tensor.transpose(xt[:, j, :], x_of[c][:, j, i * P : (i + 1) * P], ident_bf[:])
+                xt_of[c].append(xt)
+
         def pixel_norms(c):
-            ss = small.tile([P, 2], F32)
-            xt = ps_xt.tile([P, PACK, P], F32)
-            words = x_of[c][:].bitcast(F32)
-            for j in range(PACK):
-                nc.tensor.transpose(xt[:, j, :], words[:, j, :], ident_f32[:])
-            halves = xt[:].bitcast(BF16).rearrange("m j (p e) -> m e j p", e=2)
-            for e in range(2):
-                junk = junk_pool.tile([P, PACK, P], BF16, tag="junk")
+            ss = small.tile([P, CHUNK_TILES], F32)
+            for i in range(CHUNK_TILES):
+                junk = junk_pool.tile([P, CHANNELS], BF16, tag="junk")
                 nc.scalar.activation(
-                    out=junk[:], in_=halves[:, e, :, :], func=ACT.Square, accum_out=ss[:, e : e + 1]
+                    out=junk[:],
+                    in_=xt_of[c][i][:].rearrange("m j p -> m (j p)"),
+                    func=ACT.Square,
+                    accum_out=ss[:, i : i + 1],
                 )
             rn = small.tile([P, CHUNK_TILES], F32)
             nc.scalar.activation(out=rn[:], in_=ss[:], func=ACT.Abs_reciprocal_sqrt, bias=EPS)
             rn_of[c] = rn
 
         def spread(c):
-            bc = ps_bc.tile([P, 2, P], F32)
-            for e in range(2):
-                nc.tensor.transpose(bc[:, e, :], rn_of[c][:, e : e + 1].to_broadcast([P, P]), ident_f32[:])
+            bc = ps_bc.tile([P, CHUNK], F32)
+            for i in range(CHUNK_TILES):
+                nc.tensor.transpose(
+                    bc[:, i * P : (i + 1) * P], rn_of[c][:, i : i + 1].to_broadcast([P, P]), ident_f32[:]
+                )
             bc_of[c] = bc
-
-        def normalise(c):
+            bc_tail = small.tile([P, GPSIMD_PIXELS], F32)
+            nc.scalar.copy(out=bc_tail[:], in_=bc[:, VECTOR_PIXELS:CHUNK])
             grouped = work.tile([P, CHUNK, PACK], BF16, align_bytes=64)
-            nc.vector.tensor_tensor(
-                out=grouped[:].rearrange("p (m e) j -> p m e j", e=2),
-                in0=x_of[c][:].rearrange("p j (m e) -> p m e j", e=2),
-                in1=bc_of[c][:].rearrange("p e m -> p m e").unsqueeze(3).to_broadcast([P, P, 2, PACK]),
+            nc.gpsimd.tensor_tensor(
+                out=grouped[:, VECTOR_PIXELS:CHUNK, :],
+                in0=x_of[c][:, :, VECTOR_PIXELS:CHUNK].rearrange("p j w -> p w j"),
+                in1=bc_tail[:].unsqueeze(2).to_broadcast([P, GPSIMD_PIXELS, PACK]),
                 op=ALU.mult,
             )
             grouped_of[c] = grouped
+
+        def normalise(c):
+            nc.vector.tensor_tensor(
+                out=grouped_of[c][:, 0:VECTOR_PIXELS, :],
+                in0=x_of[c][:, :, 0:VECTOR_PIXELS].rearrange("p j w -> p w j"),
+                in1=bc_of[c][:, 0:VECTOR_PIXELS].unsqueeze(2).to_broadcast([P, VECTOR_PIXELS, PACK]),
+                op=ALU.mult,
+            )
 
         def quantise_and_multiply(c):
             codes = work.tile([P, CHUNK], U32, align_bytes=64)
@@ -147,23 +166,28 @@ def tile_freedamasker_s_kernel(tc, image_feat, proto_emb, out_0, out_1):
             op0=ALU.mult,
         )
 
+        transpose_pixels(0)
         pixel_norms(0)
-        pixel_norms(1)
+        transpose_pixels(1)
         pro_t = ps_misc.tile([P, PACK, P], BF16, tag="misc")
         for t in range(PACK):
             nc.tensor.transpose(pro_t[:, t, :], pro_unit[:, t, :], ident_bf[:])
         spread(0)
+        pixel_norms(1)
+        transpose_pixels(2)
+        pixel_norms(2)
 
         pro_grouped = keep.tile([P, P, PACK], BF16, align_bytes=64)
         pro_codes = keep.tile([P, PROTOS], U32, align_bytes=64)
         pro_scales = keep.tile([P, PROTOS], U8, align_bytes=64)
 
         for r in range(n_chunks):
-            if r + 2 < n_chunks:
-                pixel_norms(r + 2)
-            normalise(r)
             if r + 1 < n_chunks:
                 spread(r + 1)
+            if r + 3 < n_chunks:
+                transpose_pixels(r + 3)
+                pixel_norms(r + 3)
+            normalise(r)
             if r == 0:
                 nc.vector.tensor_copy(out=pro_grouped[:], in_=pro_t[:].rearrange("p t m -> p m t"))
                 nc.vector.quantize_mx(

@@ -22,6 +22,7 @@ PER_CLASS = 32
 PROTOS = CLASSES * PER_CLASS
 TILES_PER_IMAGE = PIXELS // P
 CHUNK_TILES = 2
+PAIR = 2
 CHUNK = CHUNK_TILES * P
 GPSIMD_PIXELS = 64
 VECTOR_PIXELS = CHUNK - GPSIMD_PIXELS
@@ -55,8 +56,6 @@ def tile_freedamasker_s_kernel(tc, image_feat, proto_emb, out_0, out_1):
             nc.sync.dma_start(out=x_sb[:], in_=src[:, :, w0 : w0 + CHUNK])
             x_of.append(x_sb)
 
-        ident_bf = const.tile([P, P], BF16)
-        make_identity(nc, ident_bf[:])
         ident_f32 = const.tile([P, P], F32)
         make_identity(nc, ident_f32[:])
         one = const.tile([P, 1], F32)
@@ -73,50 +72,48 @@ def tile_freedamasker_s_kernel(tc, image_feat, proto_emb, out_0, out_1):
         sim_of = {}
 
         def transpose_pixels(c):
-            xt_of[c] = []
-            for i in range(CHUNK_TILES):
-                xt = ps_xt.tile([P, PACK, P], BF16)
-                for j in range(PACK):
-                    nc.tensor.transpose(xt[:, j, :], x_of[c][:, j, i * P : (i + 1) * P], ident_bf[:])
-                xt_of[c].append(xt)
+            xt = ps_xt.tile([P, PACK, P], F32)
+            for j in range(PACK):
+                nc.tensor.transpose(xt[:, j, :], x_of[c][:, j, :].bitcast(F32), ident_f32[:])
+            xt_of[c] = xt[:].rearrange("w j p -> w (j p)").bitcast(BF16).rearrange("w (q e) -> w e q", e=PAIR)
 
         def pixel_norms(c):
-            ss = small.tile([P, CHUNK_TILES], F32)
-            for i in range(CHUNK_TILES):
+            ss = small.tile([P, PAIR], F32)
+            for i in range(PAIR):
                 junk = junk_pool.tile([P, CHANNELS], BF16, tag="junk")
                 nc.scalar.activation(
                     out=junk[:],
-                    in_=xt_of[c][i][:].rearrange("m j p -> m (j p)"),
+                    in_=xt_of[c][:, i, :],
                     func=ACT.Square,
                     accum_out=ss[:, i : i + 1],
                 )
-            rn = small.tile([P, CHUNK_TILES], F32)
+            rn = small.tile([P, PAIR], F32)
             nc.scalar.activation(out=rn[:], in_=ss[:], func=ACT.Abs_reciprocal_sqrt, bias=EPS)
             rn_of[c] = rn
 
         def spread(c):
-            bc = ps_bc.tile([P, CHUNK], F32)
-            for i in range(CHUNK_TILES):
-                nc.tensor.transpose(
-                    bc[:, i * P : (i + 1) * P], rn_of[c][:, i : i + 1].to_broadcast([P, P]), ident_f32[:]
-                )
-            bc_of[c] = bc
-            bc_tail = small.tile([P, GPSIMD_PIXELS], F32)
-            nc.scalar.copy(out=bc_tail[:], in_=bc[:, VECTOR_PIXELS:CHUNK])
+            bc = ps_bc.tile([P, PAIR, P], F32)
+            for e in range(PAIR):
+                nc.tensor.transpose(bc[:, e, :], rn_of[c][:, e : e + 1].to_broadcast([P, P]), ident_f32[:])
+            bc_of[c] = bc[:].rearrange("p e w -> p w e")
+            bc_tail = small.tile([P, GPSIMD_PIXELS // PAIR, PAIR], F32)
+            nc.scalar.copy(out=bc_tail[:], in_=bc_of[c][:, VECTOR_PIXELS // PAIR : P, :])
             grouped = work.tile([P, CHUNK, PACK], BF16, align_bytes=64)
             nc.gpsimd.tensor_tensor(
                 out=grouped[:, VECTOR_PIXELS:CHUNK, :],
                 in0=x_of[c][:, :, VECTOR_PIXELS:CHUNK].rearrange("p j w -> p w j"),
-                in1=bc_tail[:].unsqueeze(2).to_broadcast([P, GPSIMD_PIXELS, PACK]),
+                in1=bc_tail[:].rearrange("p w e -> p (w e)").unsqueeze(2).to_broadcast([P, GPSIMD_PIXELS, PACK]),
                 op=ALU.mult,
             )
             grouped_of[c] = grouped
 
         def normalise(c):
             nc.vector.tensor_tensor(
-                out=grouped_of[c][:, 0:VECTOR_PIXELS, :],
-                in0=x_of[c][:, :, 0:VECTOR_PIXELS].rearrange("p j w -> p w j"),
-                in1=bc_of[c][:, 0:VECTOR_PIXELS].unsqueeze(2).to_broadcast([P, VECTOR_PIXELS, PACK]),
+                out=grouped_of[c][:, 0:VECTOR_PIXELS, :].rearrange("p (w e) j -> p w e j", e=PAIR),
+                in0=x_of[c][:, :, 0:VECTOR_PIXELS].rearrange("p j (w e) -> p w e j", e=PAIR),
+                in1=bc_of[c][:, 0 : VECTOR_PIXELS // PAIR, :]
+                .unsqueeze(3)
+                .to_broadcast([P, VECTOR_PIXELS // PAIR, PAIR, PACK]),
                 op=ALU.mult,
             )
 
@@ -157,10 +154,10 @@ def tile_freedamasker_s_kernel(tc, image_feat, proto_emb, out_0, out_1):
         nc.scalar.activation(out=pro_junk[:], in_=pro_raw[:], func=ACT.Square, accum_out=pro_ss[:])
         pro_rn = small.tile([P, 1], F32)
         nc.scalar.activation(out=pro_rn[:], in_=pro_ss[:], func=ACT.Abs_reciprocal_sqrt, bias=EPS)
-        pro_unit = keep.tile([P, PACK, P], BF16)
+        pro_unit = keep.tile([P, CHANNELS], BF16)
         nc.vector.tensor_scalar(
             out=pro_unit[:],
-            in0=pro_raw[:].rearrange("m (p t) -> m t p", t=PACK),
+            in0=pro_raw[:],
             scalar1=pro_rn[:, 0:1],
             scalar2=None,
             op0=ALU.mult,
@@ -169,9 +166,10 @@ def tile_freedamasker_s_kernel(tc, image_feat, proto_emb, out_0, out_1):
         transpose_pixels(0)
         pixel_norms(0)
         transpose_pixels(1)
-        pro_t = ps_misc.tile([P, PACK, P], BF16, tag="misc")
-        for t in range(PACK):
-            nc.tensor.transpose(pro_t[:, t, :], pro_unit[:, t, :], ident_bf[:])
+        pro_words = pro_unit[:].bitcast(F32)
+        pro_t = ps_misc.tile([P, PAIR, P], F32, tag="misc")
+        for u in range(PAIR):
+            nc.tensor.transpose(pro_t[:, u, :], pro_words[:, u : CHANNELS // PAIR : PAIR], ident_f32[:])
         spread(0)
         pixel_norms(1)
         transpose_pixels(2)
@@ -189,7 +187,10 @@ def tile_freedamasker_s_kernel(tc, image_feat, proto_emb, out_0, out_1):
                 pixel_norms(r + 3)
             normalise(r)
             if r == 0:
-                nc.vector.tensor_copy(out=pro_grouped[:], in_=pro_t[:].rearrange("p t m -> p m t"))
+                nc.vector.tensor_copy(
+                    out=pro_grouped[:].rearrange("p m t -> p (m t)").bitcast(F32),
+                    in_=pro_t[:].rearrange("p u m -> p m u"),
+                )
                 nc.vector.quantize_mx(
                     out=pro_codes[:].bitcast(FP8X4),
                     scales=pro_scales[:],

@@ -14,6 +14,7 @@ AXIS_X = mybir.AxisListType.X
 
 P = 128
 PACK = 4
+PAIR = 2
 BATCH = 2
 CHANNELS = P * PACK
 PIXELS = 1024
@@ -21,11 +22,9 @@ CLASSES = 4
 PER_CLASS = 32
 PROTOS = CLASSES * PER_CLASS
 TILES_PER_IMAGE = PIXELS // P
-CHUNK_TILES = 2
-PAIR = 2
-CHUNK = CHUNK_TILES * P
-GPSIMD_PIXELS = 64
-VECTOR_PIXELS = CHUNK - GPSIMD_PIXELS
+GROUP = PAIR * P
+CHUNKS_OF_IMAGE = [[1, 1, 2], [2, 1, 1]]
+GPSIMD_PIXELS = 96
 EPS = 1e-12
 
 FLOPS = 2 * PROTOS * CHANNELS * BATCH * PIXELS
@@ -40,6 +39,7 @@ def tile_freedamasker_s_kernel(tc, image_feat, proto_emb, out_0, out_1):
         junk_pool = ctx.enter_context(tc.tile_pool(name="junk", bufs=4))
         small = ctx.enter_context(tc.tile_pool(name="small", bufs=4))
         work = ctx.enter_context(tc.tile_pool(name="work", bufs=3))
+        group_pool = ctx.enter_context(tc.tile_pool(name="group_pool", bufs=1))
         ps_xt = ctx.enter_context(tc.psum_pool(name="ps_xt", bufs=3))
         ps_bc = ctx.enter_context(tc.psum_pool(name="ps_bc", bufs=2))
         ps_sim = ctx.enter_context(tc.psum_pool(name="ps_sim", bufs=2))
@@ -47,13 +47,23 @@ def tile_freedamasker_s_kernel(tc, image_feat, proto_emb, out_0, out_1):
 
         pro_raw = keep.tile([P, CHANNELS], BF16)
         nc.scalar.dma_start(out=pro_raw[:], in_=proto_emb.rearrange("n k c -> (n k) c"))
-        chunks = [(b, w0) for b in range(BATCH) for w0 in range(0, PIXELS, CHUNK)]
+        chunks = []
+        group_of = []
+        for b in range(BATCH):
+            w0 = 0
+            for groups in CHUNKS_OF_IMAGE[b]:
+                for g in range(groups):
+                    group_of.append((len(chunks), g))
+                chunks.append((b, w0, groups, groups * (GROUP - (GPSIMD_PIXELS if chunks else 0))))
+                w0 += groups * GROUP
         n_chunks = len(chunks)
+        n_groups = len(group_of)
+        last_group = [max(q for q in range(n_groups) if group_of[q][0] == c) for c in range(n_chunks)]
         x_of = []
-        for b, w0 in chunks:
-            x_sb = keep.tile([P, PACK, CHUNK], BF16, name="x_%d_%d" % (b, w0))
+        for b, w0, groups, vec in chunks:
+            x_sb = keep.tile([P, PACK, groups * GROUP], BF16, name="x_%d_%d" % (b, w0))
             src = image_feat[b].rearrange("(p j) h w -> p j (h w)", j=PACK)
-            nc.sync.dma_start(out=x_sb[:], in_=src[:, :, w0 : w0 + CHUNK])
+            nc.sync.dma_start(out=x_sb[:], in_=src[:, :, w0 : w0 + groups * GROUP])
             x_of.append(x_sb)
 
         ident_f32 = const.tile([P, P], F32)
@@ -66,67 +76,85 @@ def tile_freedamasker_s_kernel(tc, image_feat, proto_emb, out_0, out_1):
         best = keep.tile([P, BATCH, CLASSES, TILES_PER_IMAGE], F32)
         total = keep.tile([P, BATCH, CLASSES, TILES_PER_IMAGE], F32)
         xt_of = {}
+        ss_of = {}
         rn_of = {}
         bc_of = {}
+        bc_tail_of = {}
         grouped_of = {}
         sim_of = {}
 
-        def transpose_pixels(c):
+        def transpose_group(q):
+            c, g = group_of[q]
             xt = ps_xt.tile([P, PACK, P], F32)
             for j in range(PACK):
-                nc.tensor.transpose(xt[:, j, :], x_of[c][:, j, :].bitcast(F32), ident_f32[:])
-            xt_of[c] = xt[:].rearrange("w j p -> w (j p)").bitcast(BF16).rearrange("w (q e) -> w e q", e=PAIR)
+                words = x_of[c][:, j, g * GROUP : (g + 1) * GROUP].bitcast(F32)
+                nc.tensor.transpose(xt[:, j, :], words, ident_f32[:])
+            xt_of[q] = xt[:].rearrange("w j p -> w (j p)").bitcast(BF16).rearrange("w (q e) -> w e q", e=PAIR)
 
-        def pixel_norms(c):
-            ss = small.tile([P, PAIR], F32)
-            for i in range(PAIR):
+        def norm_group(q):
+            c, g = group_of[q]
+            groups = chunks[c][2]
+            if g == 0:
+                ss = small.tile([P, groups, PAIR], F32)
+                ss_of[c] = ss
+            for e in range(PAIR):
                 junk = junk_pool.tile([P, CHANNELS], BF16, tag="junk")
                 nc.scalar.activation(
-                    out=junk[:],
-                    in_=xt_of[c][:, i, :],
-                    func=ACT.Square,
-                    accum_out=ss[:, i : i + 1],
+                    out=junk[:], in_=xt_of[q][:, e, :], func=ACT.Square, accum_out=ss_of[c][:, g, e : e + 1]
                 )
-            rn = small.tile([P, PAIR], F32)
-            nc.scalar.activation(out=rn[:], in_=ss[:], func=ACT.Abs_reciprocal_sqrt, bias=EPS)
-            rn_of[c] = rn
+            if g == groups - 1:
+                rn = small.tile([P, groups, PAIR], F32)
+                nc.scalar.activation(out=rn[:], in_=ss_of[c][:], func=ACT.Abs_reciprocal_sqrt, bias=EPS)
+                rn_of[c] = rn
 
         def spread(c):
-            bc = ps_bc.tile([P, PAIR, P], F32)
-            for e in range(PAIR):
-                nc.tensor.transpose(bc[:, e, :], rn_of[c][:, e : e + 1].to_broadcast([P, P]), ident_f32[:])
+            groups = chunks[c][2]
+            bc = ps_bc.tile([P, PAIR, groups * P], F32)
+            for g in range(groups):
+                for e in range(PAIR):
+                    nc.tensor.transpose(
+                        bc[:, e, g * P : (g + 1) * P],
+                        rn_of[c][:, g, e : e + 1].to_broadcast([P, P]),
+                        ident_f32[:],
+                    )
             bc_of[c] = bc[:].rearrange("p e w -> p w e")
-            bc_tail = small.tile([P, GPSIMD_PIXELS // PAIR, PAIR], F32)
-            nc.scalar.copy(out=bc_tail[:], in_=bc_of[c][:, VECTOR_PIXELS // PAIR : P, :])
-            grouped = work.tile([P, CHUNK, PACK], BF16, align_bytes=64)
+
+        def copy_factors_for_gpsimd(c):
+            b, w0, groups, vec = chunks[c]
+            bc_tail = small.tile([P, groups * P - vec // PAIR, PAIR], F32)
+            nc.scalar.copy(out=bc_tail[:], in_=bc_of[c][:, vec // PAIR : groups * P, :])
+            bc_tail_of[c] = bc_tail
+
+        def normalise_on_gpsimd(c):
+            b, w0, groups, vec = chunks[c]
+            pixels = groups * GROUP - vec
             nc.gpsimd.tensor_tensor(
-                out=grouped[:, VECTOR_PIXELS:CHUNK, :],
-                in0=x_of[c][:, :, VECTOR_PIXELS:CHUNK].rearrange("p j w -> p w j"),
-                in1=bc_tail[:].rearrange("p w e -> p (w e)").unsqueeze(2).to_broadcast([P, GPSIMD_PIXELS, PACK]),
+                out=grouped_of[c][:, vec : groups * GROUP, :],
+                in0=x_of[c][:, :, vec : groups * GROUP].rearrange("p j w -> p w j"),
+                in1=bc_tail_of[c][:].rearrange("p w e -> p (w e)").unsqueeze(2).to_broadcast([P, pixels, PACK]),
                 op=ALU.mult,
             )
-            grouped_of[c] = grouped
 
-        def normalise(c):
+        def normalise_on_vector(c):
+            vec = chunks[c][3]
             nc.vector.tensor_tensor(
-                out=grouped_of[c][:, 0:VECTOR_PIXELS, :].rearrange("p (w e) j -> p w e j", e=PAIR),
-                in0=x_of[c][:, :, 0:VECTOR_PIXELS].rearrange("p j (w e) -> p w e j", e=PAIR),
-                in1=bc_of[c][:, 0 : VECTOR_PIXELS // PAIR, :]
-                .unsqueeze(3)
-                .to_broadcast([P, VECTOR_PIXELS // PAIR, PAIR, PACK]),
+                out=grouped_of[c][:, 0:vec, :].rearrange("p (w e) j -> p w e j", e=PAIR),
+                in0=x_of[c][:, :, 0:vec].rearrange("p j (w e) -> p w e j", e=PAIR),
+                in1=bc_of[c][:, 0 : vec // PAIR, :].unsqueeze(3).to_broadcast([P, vec // PAIR, PAIR, PACK]),
                 op=ALU.mult,
             )
 
         def quantise_and_multiply(c):
-            codes = work.tile([P, CHUNK], U32, align_bytes=64)
-            scales = work.tile([P, CHUNK], U8, align_bytes=64)
+            tiles = PAIR * chunks[c][2]
+            codes = work.tile([P, tiles * P], U32, align_bytes=64)
+            scales = work.tile([P, tiles * P], U8, align_bytes=64)
             nc.vector.quantize_mx(
                 out=codes[:].bitcast(FP8X4),
                 scales=scales[:],
                 in_=grouped_of[c][:].rearrange("p w j -> p (w j)"),
             )
-            sim = ps_sim.tile([P, CHUNK_TILES, PROTOS], F32)
-            for i in range(CHUNK_TILES):
+            sim = ps_sim.tile([P, tiles, PROTOS], F32)
+            for i in range(tiles):
                 cols = slice(i * P, (i + 1) * P)
                 nc.tensor.matmul_mx(
                     out=sim[:, i, :],
@@ -140,10 +168,10 @@ def tile_freedamasker_s_kernel(tc, image_feat, proto_emb, out_0, out_1):
             sim_of[c] = sim
 
         def reduce_over_prototypes(c, op, into):
-            b, w0 = chunks[c]
+            b, w0, groups, vec = chunks[c]
             t0 = w0 // P
             nc.vector.tensor_reduce(
-                out=into[:, b, :, t0 : t0 + CHUNK_TILES].rearrange("m n i -> m i n"),
+                out=into[:, b, :, t0 : t0 + PAIR * groups].rearrange("m n i -> m i n"),
                 in_=sim_of[c][:].rearrange("m i (n k) -> m i n k", k=PER_CLASS),
                 axis=AXIS_X,
                 op=op,
@@ -163,17 +191,18 @@ def tile_freedamasker_s_kernel(tc, image_feat, proto_emb, out_0, out_1):
             op0=ALU.mult,
         )
 
-        transpose_pixels(0)
-        pixel_norms(0)
-        transpose_pixels(1)
+        transpose_group(0)
+        norm_group(0)
+        transpose_group(1)
+        norm_group(1)
+        spread(0)
         pro_words = pro_unit[:].bitcast(F32)
         pro_t = ps_misc.tile([P, PAIR, P], F32, tag="misc")
         for u in range(PAIR):
             nc.tensor.transpose(pro_t[:, u, :], pro_words[:, u : CHANNELS // PAIR : PAIR], ident_f32[:])
-        spread(0)
-        pixel_norms(1)
-        transpose_pixels(2)
-        pixel_norms(2)
+        transpose_group(2)
+        next_transpose = 3
+        next_norm = 2
 
         pro_grouped = keep.tile([P, P, PACK], BF16, align_bytes=64)
         pro_codes = keep.tile([P, PROTOS], U32, align_bytes=64)
@@ -181,11 +210,19 @@ def tile_freedamasker_s_kernel(tc, image_feat, proto_emb, out_0, out_1):
 
         for r in range(n_chunks):
             if r + 1 < n_chunks:
+                while next_norm <= min(last_group[r + 1] + 1, n_groups - 1):
+                    norm_group(next_norm)
+                    next_norm += 1
+                    if next_transpose < n_groups:
+                        transpose_group(next_transpose)
+                        next_transpose += 1
                 spread(r + 1)
-            if r + 3 < n_chunks:
-                transpose_pixels(r + 3)
-                pixel_norms(r + 3)
-            normalise(r)
+                copy_factors_for_gpsimd(r + 1)
+            grouped = group_pool.tile([P, chunks[r][2] * GROUP, PACK], BF16, align_bytes=64)
+            grouped_of[r] = grouped
+            if r > 0:
+                normalise_on_gpsimd(r)
+            normalise_on_vector(r)
             if r == 0:
                 nc.vector.tensor_copy(
                     out=pro_grouped[:].rearrange("p m t -> p (m t)").bitcast(F32),
@@ -205,7 +242,7 @@ def tile_freedamasker_s_kernel(tc, image_feat, proto_emb, out_0, out_1):
         reduce_over_prototypes(n_chunks - 1, ALU.add, total)
 
         warm2 = const.tile([P, 1], F32)
-        nc.scalar.activation(out=warm2[:], in_=rn_of[n_chunks - 1][:, 0:1], func=ACT.Sigmoid)
+        nc.scalar.activation(out=warm2[:], in_=rn_of[n_chunks - 1][:, 0, 0:1], func=ACT.Sigmoid)
 
         half = BATCH * CLASSES * TILES_PER_IMAGE
         both = keep.tile([P, 2, half], F32)

@@ -23,8 +23,10 @@ PER_CLASS = 32
 PROTOS = CLASSES * PER_CLASS
 TILES_PER_IMAGE = PIXELS // P
 GROUP = PAIR * P
-CHUNKS_OF_IMAGE = [[1, 1, 2], [2, 1, 1]]
-GPSIMD_PIXELS = 96
+CHUNKS_OF_IMAGE = [
+    [(P, 0), (P, 0), (GROUP, 0), (GROUP, 64), (GROUP, 96)],
+    [(2 * GROUP, 208), (GROUP, 128), (GROUP, 96)],
+]
 EPS = 1e-12
 
 FLOPS = 2 * PROTOS * CHANNELS * BATCH * PIXELS
@@ -48,26 +50,23 @@ def tile_freedamasker_s_kernel(tc, image_feat, proto_emb, out_0, out_1):
         pro_raw = keep.tile([P, CHANNELS], BF16)
         nc.scalar.dma_start(out=pro_raw[:], in_=proto_emb.rearrange("n k c -> (n k) c"))
         chunks = []
-        group_of = []
         for b in range(BATCH):
             w0 = 0
-            for groups in CHUNKS_OF_IMAGE[b]:
-                for g in range(groups):
-                    group_of.append((len(chunks), g))
-                chunks.append((b, w0, groups, groups * (GROUP - (GPSIMD_PIXELS if chunks else 0))))
-                w0 += groups * GROUP
+            for pixels, gpsimd_pixels in CHUNKS_OF_IMAGE[b]:
+                chunks.append((b, w0, pixels, pixels - gpsimd_pixels))
+                w0 += pixels
         n_chunks = len(chunks)
-        n_groups = len(group_of)
-        last_group = [max(q for q in range(n_groups) if group_of[q][0] == c) for c in range(n_chunks)]
         x_of = []
-        for b, w0, groups, vec in chunks:
-            x_sb = keep.tile([P, PACK, groups * GROUP], BF16, name="x_%d_%d" % (b, w0))
+        for b, w0, pixels, vec in chunks:
+            x_sb = keep.tile([P, PACK, pixels], BF16, name="x_%d_%d" % (b, w0))
             src = image_feat[b].rearrange("(p j) h w -> p j (h w)", j=PACK)
-            nc.sync.dma_start(out=x_sb[:], in_=src[:, :, w0 : w0 + groups * GROUP])
+            nc.sync.dma_start(out=x_sb[:], in_=src[:, :, w0 : w0 + pixels])
             x_of.append(x_sb)
 
         ident_f32 = const.tile([P, P], F32)
         make_identity(nc, ident_f32[:])
+        ident_bf = const.tile([P, P], BF16)
+        make_identity(nc, ident_bf[:])
         one = const.tile([P, 1], F32)
         nc.vector.memset(one[:], 1.0)
         warm = const.tile([P, 1], F32)
@@ -83,69 +82,94 @@ def tile_freedamasker_s_kernel(tc, image_feat, proto_emb, out_0, out_1):
         grouped_of = {}
         sim_of = {}
 
-        def transpose_group(q):
-            c, g = group_of[q]
-            xt = ps_xt.tile([P, PACK, P], F32)
-            for j in range(PACK):
-                words = x_of[c][:, j, g * GROUP : (g + 1) * GROUP].bitcast(F32)
-                nc.tensor.transpose(xt[:, j, :], words, ident_f32[:])
-            xt_of[q] = xt[:].rearrange("w j p -> w (j p)").bitcast(BF16).rearrange("w (q e) -> w e q", e=PAIR)
-
-        def norm_group(q):
-            c, g = group_of[q]
-            groups = chunks[c][2]
-            if g == 0:
-                ss = small.tile([P, groups, PAIR], F32)
-                ss_of[c] = ss
+        blocks = [(1, 0)]
+        for c in range(2, n_chunks):
+            for g in range(chunks[c][2] // GROUP):
+                blocks.append((c, g))
+        steps = [(0, 0)]
+        for q in range(1, len(blocks)):
             for e in range(PAIR):
-                junk = junk_pool.tile([P, CHANNELS], BF16, tag="junk")
-                nc.scalar.activation(
-                    out=junk[:], in_=xt_of[q][:, e, :], func=ACT.Square, accum_out=ss_of[c][:, g, e : e + 1]
-                )
-            if g == groups - 1:
-                rn = small.tile([P, groups, PAIR], F32)
-                nc.scalar.activation(out=rn[:], in_=ss_of[c][:], func=ACT.Abs_reciprocal_sqrt, bias=EPS)
-                rn_of[c] = rn
+                steps.append((q, e))
+        last_step = {}
+        for s in range(len(steps)):
+            last_step[blocks[steps[s][0]][0]] = s
+
+        def transpose_block(q):
+            c, g = blocks[q]
+            if chunks[c][2] == P:
+                xt = ps_xt.tile([P, PACK, P], BF16)
+                for j in range(PACK):
+                    nc.tensor.transpose(xt[:, j, :], x_of[c][:, j, :], ident_bf[:])
+                xt_of[q] = xt[:].rearrange("w j p -> w (j p)").unsqueeze(1)
+            else:
+                xt = ps_xt.tile([P, PACK, P], F32)
+                for j in range(PACK):
+                    words = x_of[c][:, j, g * GROUP : (g + 1) * GROUP].bitcast(F32)
+                    nc.tensor.transpose(xt[:, j, :], words, ident_f32[:])
+                xt_of[q] = xt[:].rearrange("w j p -> w (j p)").bitcast(BF16).rearrange("w (q e) -> w e q", e=PAIR)
+
+        def inverse_norm(c):
+            rn = small.tile([P, chunks[c][2] // P], F32)
+            nc.scalar.activation(out=rn[:], in_=ss_of[c][:], func=ACT.Abs_reciprocal_sqrt, bias=EPS)
+            rn_of[c] = rn
+
+        def square_step(s):
+            q, e = steps[s]
+            c, g = blocks[q]
+            if g == 0 and e == 0:
+                ss = small.tile([P, chunks[c][2] // P], F32)
+                ss_of[c] = ss
+            i = PAIR * g + e
+            junk = junk_pool.tile([P, CHANNELS], BF16, tag="junk")
+            nc.scalar.activation(
+                out=junk[:], in_=xt_of[q][:, e, :], func=ACT.Square, accum_out=ss_of[c][:, i : i + 1]
+            )
+            if s == last_step[c]:
+                inverse_norm(c)
+            if e == 0 and q + 2 < len(blocks):
+                transpose_block(q + 2)
 
         def spread(c):
-            groups = chunks[c][2]
-            bc = ps_bc.tile([P, PAIR, groups * P], F32)
-            for g in range(groups):
-                for e in range(PAIR):
-                    nc.tensor.transpose(
-                        bc[:, e, g * P : (g + 1) * P],
-                        rn_of[c][:, g, e : e + 1].to_broadcast([P, P]),
-                        ident_f32[:],
-                    )
+            tiles = chunks[c][2] // P
+            pair = min(tiles, PAIR)
+            bc = ps_bc.tile([P, pair, tiles // pair * P], F32)
+            for i in range(tiles):
+                g, e = divmod(i, pair)
+                nc.tensor.transpose(
+                    bc[:, e, g * P : (g + 1) * P], rn_of[c][:, i : i + 1].to_broadcast([P, P]), ident_f32[:]
+                )
             bc_of[c] = bc[:].rearrange("p e w -> p w e")
 
         def copy_factors_for_gpsimd(c):
-            b, w0, groups, vec = chunks[c]
-            bc_tail = small.tile([P, groups * P - vec // PAIR, PAIR], F32)
-            nc.scalar.copy(out=bc_tail[:], in_=bc_of[c][:, vec // PAIR : groups * P, :])
+            b, w0, pixels, vec = chunks[c]
+            bc_tail = small.tile([P, (pixels - vec) // PAIR, PAIR], F32)
+            nc.scalar.copy(out=bc_tail[:], in_=bc_of[c][:, vec // PAIR : pixels // PAIR, :])
             bc_tail_of[c] = bc_tail
 
         def normalise_on_gpsimd(c):
-            b, w0, groups, vec = chunks[c]
-            pixels = groups * GROUP - vec
+            b, w0, pixels, vec = chunks[c]
             nc.gpsimd.tensor_tensor(
-                out=grouped_of[c][:, vec : groups * GROUP, :],
-                in0=x_of[c][:, :, vec : groups * GROUP].rearrange("p j w -> p w j"),
-                in1=bc_tail_of[c][:].rearrange("p w e -> p (w e)").unsqueeze(2).to_broadcast([P, pixels, PACK]),
+                out=grouped_of[c][:, vec:pixels, :],
+                in0=x_of[c][:, :, vec:pixels].rearrange("p j w -> p w j"),
+                in1=bc_tail_of[c][:]
+                .rearrange("p w e -> p (w e)")
+                .unsqueeze(2)
+                .to_broadcast([P, pixels - vec, PACK]),
                 op=ALU.mult,
             )
 
         def normalise_on_vector(c):
-            vec = chunks[c][3]
+            b, w0, pixels, vec = chunks[c]
+            pair = min(pixels // P, PAIR)
             nc.vector.tensor_tensor(
-                out=grouped_of[c][:, 0:vec, :].rearrange("p (w e) j -> p w e j", e=PAIR),
-                in0=x_of[c][:, :, 0:vec].rearrange("p j (w e) -> p w e j", e=PAIR),
-                in1=bc_of[c][:, 0 : vec // PAIR, :].unsqueeze(3).to_broadcast([P, vec // PAIR, PAIR, PACK]),
+                out=grouped_of[c][:, 0:vec, :].rearrange("p (w e) j -> p w e j", e=pair),
+                in0=x_of[c][:, :, 0:vec].rearrange("p j (w e) -> p w e j", e=pair),
+                in1=bc_of[c][:, 0 : vec // pair, :].unsqueeze(3).to_broadcast([P, vec // pair, pair, PACK]),
                 op=ALU.mult,
             )
 
         def quantise_and_multiply(c):
-            tiles = PAIR * chunks[c][2]
+            tiles = chunks[c][2] // P
             codes = work.tile([P, tiles * P], U32, align_bytes=64)
             scales = work.tile([P, tiles * P], U8, align_bytes=64)
             nc.vector.quantize_mx(
@@ -168,10 +192,10 @@ def tile_freedamasker_s_kernel(tc, image_feat, proto_emb, out_0, out_1):
             sim_of[c] = sim
 
         def reduce_over_prototypes(c, op, into):
-            b, w0, groups, vec = chunks[c]
+            b, w0, pixels, vec = chunks[c]
             t0 = w0 // P
             nc.vector.tensor_reduce(
-                out=into[:, b, :, t0 : t0 + PAIR * groups].rearrange("m n i -> m i n"),
+                out=into[:, b, :, t0 : t0 + pixels // P].rearrange("m n i -> m i n"),
                 in_=sim_of[c][:].rearrange("m i (n k) -> m i n k", k=PER_CLASS),
                 axis=AXIS_X,
                 op=op,
@@ -182,6 +206,25 @@ def tile_freedamasker_s_kernel(tc, image_feat, proto_emb, out_0, out_1):
         nc.scalar.activation(out=pro_junk[:], in_=pro_raw[:], func=ACT.Square, accum_out=pro_ss[:])
         pro_rn = small.tile([P, 1], F32)
         nc.scalar.activation(out=pro_rn[:], in_=pro_ss[:], func=ACT.Abs_reciprocal_sqrt, bias=EPS)
+
+        gram = ps_sim.tile([P, P], F32, tag="sim")
+        for j in range(PACK):
+            nc.tensor.matmul(
+                gram[:], lhsT=x_of[0][:, j, :], rhs=x_of[0][:, j, :], start=(j == 0), stop=(j == PACK - 1)
+            )
+        diagonal = keep.tile([P, P], F32)
+        ss = small.tile([P, 1], F32)
+        nc.vector.scalar_tensor_tensor(
+            out=diagonal[:],
+            in0=gram[:],
+            scalar=1.0,
+            in1=ident_f32[:],
+            op0=ALU.mult,
+            op1=ALU.mult,
+            accum_out=ss[:],
+        )
+        ss_of[0] = ss
+        inverse_norm(0)
         pro_unit = keep.tile([P, CHANNELS], BF16)
         nc.vector.tensor_scalar(
             out=pro_unit[:],
@@ -190,19 +233,14 @@ def tile_freedamasker_s_kernel(tc, image_feat, proto_emb, out_0, out_1):
             scalar2=None,
             op0=ALU.mult,
         )
-
-        transpose_group(0)
-        norm_group(0)
-        transpose_group(1)
-        norm_group(1)
+        transpose_block(0)
         spread(0)
+        transpose_block(1)
         pro_words = pro_unit[:].bitcast(F32)
         pro_t = ps_misc.tile([P, PAIR, P], F32, tag="misc")
         for u in range(PAIR):
             nc.tensor.transpose(pro_t[:, u, :], pro_words[:, u : CHANNELS // PAIR : PAIR], ident_f32[:])
-        transpose_group(2)
-        next_transpose = 3
-        next_norm = 2
+        next_step = 0
 
         pro_grouped = keep.tile([P, P, PACK], BF16, align_bytes=64)
         pro_codes = keep.tile([P, PROTOS], U32, align_bytes=64)
@@ -210,17 +248,18 @@ def tile_freedamasker_s_kernel(tc, image_feat, proto_emb, out_0, out_1):
 
         for r in range(n_chunks):
             if r + 1 < n_chunks:
-                while next_norm <= min(last_group[r + 1] + 1, n_groups - 1):
-                    norm_group(next_norm)
-                    next_norm += 1
-                    if next_transpose < n_groups:
-                        transpose_group(next_transpose)
-                        next_transpose += 1
+                while next_step <= last_step[r + 1]:
+                    square_step(next_step)
+                    next_step += 1
                 spread(r + 1)
-                copy_factors_for_gpsimd(r + 1)
-            grouped = group_pool.tile([P, chunks[r][2] * GROUP, PACK], BF16, align_bytes=64)
+                if next_step < len(steps):
+                    square_step(next_step)
+                    next_step += 1
+                if chunks[r + 1][3] < chunks[r + 1][2]:
+                    copy_factors_for_gpsimd(r + 1)
+            grouped = group_pool.tile([P, chunks[r][2], PACK], BF16, align_bytes=64)
             grouped_of[r] = grouped
-            if r > 0:
+            if chunks[r][3] < chunks[r][2]:
                 normalise_on_gpsimd(r)
             normalise_on_vector(r)
             if r == 0:
@@ -242,7 +281,7 @@ def tile_freedamasker_s_kernel(tc, image_feat, proto_emb, out_0, out_1):
         reduce_over_prototypes(n_chunks - 1, ALU.add, total)
 
         warm2 = const.tile([P, 1], F32)
-        nc.scalar.activation(out=warm2[:], in_=rn_of[n_chunks - 1][:, 0, 0:1], func=ACT.Sigmoid)
+        nc.scalar.activation(out=warm2[:], in_=rn_of[n_chunks - 1][:, 0:1], func=ACT.Sigmoid)
 
         half = BATCH * CLASSES * TILES_PER_IMAGE
         both = keep.tile([P, 2, half], F32)
@@ -254,13 +293,15 @@ def tile_freedamasker_s_kernel(tc, image_feat, proto_emb, out_0, out_1):
             op0=ALU.mult,
             op1=ALU.add,
         )
-        both_t = ps_misc.tile([P, P], F32, tag="misc")
-        nc.tensor.transpose(both_t[:], both[:].rearrange("m o c -> m (o c)"), ident_f32[:])
+        for_vector = ps_misc.tile([P, P], F32, tag="misc")
+        nc.tensor.transpose(for_vector[:], both[:].rearrange("m o c -> m (o c)"), ident_f32[:])
+        for_scalar = ps_bc.tile([P, P], F32, tag="bc")
+        nc.tensor.transpose(for_scalar[:], both[:].rearrange("m o c -> m (o c)"), ident_f32[:])
         result = keep.tile([P, P], F32)
         nc.vector.tensor_scalar(
-            out=result[0:half, :], in0=both_t[0:half, :], scalar1=0.5, scalar2=None, op0=ALU.mult
+            out=result[0:half, :], in0=for_vector[0:half, :], scalar1=0.5, scalar2=None, op0=ALU.mult
         )
-        nc.scalar.activation(out=result[half:P, :], in_=both_t[half:P, :], func=ACT.Sigmoid, scale=0.5)
+        nc.scalar.activation(out=result[half:P, :], in_=for_scalar[half:P, :], func=ACT.Sigmoid, scale=0.5)
         nc.sync.dma_start(
             out=out_1.rearrange("b n (t r) w -> (b n t) (r w)", t=TILES_PER_IMAGE), in_=result[0:half, :]
         )

@@ -24,8 +24,8 @@ PROTOS = CLASSES * PER_CLASS
 TILES_PER_IMAGE = PIXELS // P
 GROUP = PAIR * P
 CHUNKS_OF_IMAGE = [
-    [(P, 0), (P, 0), (GROUP, 0), (GROUP, 64), (GROUP, 96)],
-    [(2 * GROUP, 208), (GROUP, 128), (GROUP, 96)],
+    [(P, 0), (P, 0), (GROUP, 0), (GROUP, 64), (GROUP, 88)],
+    [(GROUP, 88), (GROUP, 88), (GROUP, 88), (GROUP, 80)],
 ]
 EPS = 1e-12
 

@@ -124,7 +124,10 @@ def tile_freedamasker_s_kernel(tc, image_feat, proto_emb, out_0, out_1):
             nc.scalar.activation(
                 out=junk[:], in_=xt_of[q][:, e, :], func=ACT.Square, accum_out=ss_of[c][:, i : i + 1]
             )
-            if s == last_step[c]:
+            late = blocks[steps[s - 1][0]][0] if s > 0 else 0
+            if late >= 4 and s - 1 == last_step[late]:
+                inverse_norm(late)
+            if s == last_step[c] and (c < 4 or c == n_chunks - 1):
                 inverse_norm(c)
             if e == 0 and q + 2 < len(blocks):
                 transpose_block(q + 2)
@@ -248,7 +251,7 @@ def tile_freedamasker_s_kernel(tc, image_feat, proto_emb, out_0, out_1):
 
         for r in range(n_chunks):
             if r + 1 < n_chunks:
-                while next_step <= last_step[r + 1]:
+                while next_step <= min(last_step[r + 1] + (1 if r + 1 >= 4 else 0), len(steps) - 1):
                     square_step(next_step)
                     next_step += 1
                 spread(r + 1)

@@ -25,8 +25,9 @@ TILES_PER_IMAGE = PIXELS // P
 GROUP = PAIR * P
 CHUNKS_OF_IMAGE = [
     [(P, 0), (P, 0), (GROUP, 0), (GROUP, 64), (GROUP, 88)],
-    [(GROUP, 88), (GROUP, 88), (GROUP, 88), (GROUP, 80)],
+    [(GROUP, 88), (GROUP, 80), (GROUP, 72), (GROUP, 80)],
 ]
+SCALAR_SUMS = (5, 6)
 EPS = 1e-12
 
 FLOPS = 2 * PROTOS * CHANNELS * BATCH * PIXELS
@@ -204,6 +205,19 @@ def tile_freedamasker_s_kernel(tc, image_feat, proto_emb, out_0, out_1):
                 op=op,
             )
 
+        def sum_on_scalar(c):
+            b, w0, pixels, vec = chunks[c]
+            for i in range(pixels // P):
+                for n in range(CLASSES):
+                    t = w0 // P + i
+                    summed = junk_pool.tile([P, PER_CLASS], F32, tag="summed")
+                    nc.scalar.activation(
+                        out=summed[:],
+                        in_=sim_of[c][:, i, n * PER_CLASS : (n + 1) * PER_CLASS],
+                        func=ACT.Copy,
+                        accum_out=total[:, b, n, t : t + 1],
+                    )
+
         pro_ss = small.tile([P, 1], F32)
         pro_junk = junk_pool.tile([P, CHANNELS], BF16, tag="junk")
         nc.scalar.activation(out=pro_junk[:], in_=pro_raw[:], func=ACT.Square, accum_out=pro_ss[:])
@@ -277,8 +291,10 @@ def tile_freedamasker_s_kernel(tc, image_feat, proto_emb, out_0, out_1):
                 )
             else:
                 reduce_over_prototypes(r - 1, ALU.max, best)
+                if r - 1 in SCALAR_SUMS:
+                    sum_on_scalar(r - 1)
             quantise_and_multiply(r)
-            if r > 0:
+            if r > 0 and r - 1 not in SCALAR_SUMS:
                 reduce_over_prototypes(r - 1, ALU.add, total)
         reduce_over_prototypes(n_chunks - 1, ALU.max, best)
         reduce_over_prototypes(n_chunks - 1, ALU.add, total)

from contextlib import ExitStack

import concourse.mybir as mybir
from concourse.masks import make_identity

BF16 = mybir.dt.bfloat16
F32 = mybir.dt.float32
U32 = mybir.dt.uint32
U8 = mybir.dt.uint8
FP8X4 = mybir.dt.float8_e4m3fn_x4
ACT = mybir.ActivationFunctionType
ALU = mybir.AluOpType
AXIS_X = mybir.AxisListType.X

P = 128
PACK = 4
PAIR = 2
BATCH = 2
CHANNELS = P * PACK
PIXELS = 1024
CLASSES = 4
PER_CLASS = 32
PROTOS = CLASSES * PER_CLASS
TILES_PER_IMAGE = PIXELS // P
GROUP = PAIR * P
CHUNKS_OF_IMAGE = [
    [(P, 0), (P, 0), (GROUP, 0), (GROUP, 64), (GROUP, 88)],
    [(GROUP, 88), (GROUP, 80), (GROUP, 72), (GROUP, 80)],
]
SCALAR_SUMS = (5, 6)
EPS = 1e-12

FLOPS = 2 * PROTOS * CHANNELS * BATCH * PIXELS


def tile_freedamasker_s_kernel(tc, image_feat, proto_emb, out_0, out_1):
    nc = tc.nc
    with ExitStack() as ctx:
        ctx.enter_context(tc.manual_schedule())
        const = ctx.enter_context(tc.tile_pool(name="const", bufs=1))
        keep = ctx.enter_context(tc.tile_pool(name="keep", bufs=1))
        junk_pool = ctx.enter_context(tc.tile_pool(name="junk", bufs=4))
        small = ctx.enter_context(tc.tile_pool(name="small", bufs=4))
        work = ctx.enter_context(tc.tile_pool(name="work", bufs=3))
        group_pool = ctx.enter_context(tc.tile_pool(name="group_pool", bufs=1))
        ps_xt = ctx.enter_context(tc.psum_pool(name="ps_xt", bufs=3))
        ps_bc = ctx.enter_context(tc.psum_pool(name="ps_bc", bufs=2))
        ps_sim = ctx.enter_context(tc.psum_pool(name="ps_sim", bufs=2))
        ps_misc = ctx.enter_context(tc.psum_pool(name="ps_misc", bufs=1))

        pro_raw = keep.tile([P, CHANNELS], BF16)
        nc.scalar.dma_start(out=pro_raw[:], in_=proto_emb.rearrange("n k c -> (n k) c"))
        chunks = []
        for b in range(BATCH):
            w0 = 0
            for pixels, gpsimd_pixels in CHUNKS_OF_IMAGE[b]:
                chunks.append((b, w0, pixels, pixels - gpsimd_pixels))
                w0 += pixels
        n_chunks = len(chunks)
        x_of = []
        for b, w0, pixels, vec in chunks:
            x_sb = keep.tile([P, PACK, pixels], BF16, name="x_%d_%d" % (b, w0))
            src = image_feat[b].rearrange("(p j) h w -> p j (h w)", j=PACK)
            nc.sync.dma_start(out=x_sb[:], in_=src[:, :, w0 : w0 + pixels])
            x_of.append(x_sb)

        ident_f32 = const.tile([P, P], F32)
        make_identity(nc, ident_f32[:])
        ident_bf = const.tile([P, P], BF16)
        make_identity(nc, ident_bf[:])
        one = const.tile([P, 1], F32)
        nc.vector.memset(one[:], 1.0)
        warm = const.tile([P, 1], F32)
        nc.scalar.activation(out=warm[:], in_=one[:], func=ACT.Abs_reciprocal_sqrt)

        best = keep.tile([P, BATCH, CLASSES, TILES_PER_IMAGE], F32)
        total = keep.tile([P, BATCH, CLASSES, TILES_PER_IMAGE], F32)
        xt_of = {}
        ss_of = {}
        rn_of = {}
        bc_of = {}
        bc_tail_of = {}
        grouped_of = {}
        sim_of = {}

        blocks = [(1, 0)]
        for c in range(2, n_chunks):
            for g in range(chunks[c][2] // GROUP):
                blocks.append((c, g))
        steps = [(0, 0)]
        for q in range(1, len(blocks)):
            for e in range(PAIR):
                steps.append((q, e))
        last_step = {}
        for s in range(len(steps)):
            last_step[blocks[steps[s][0]][0]] = s

        def transpose_block(q):
            c, g = blocks[q]
            if chunks[c][2] == P:
                xt = ps_xt.tile([P, PACK, P], BF16)
                for j in range(PACK):
                    nc.tensor.transpose(xt[:, j, :], x_of[c][:, j, :], ident_bf[:])
                xt_of[q] = xt[:].rearrange("w j p -> w (j p)").unsqueeze(1)
            else:
                xt = ps_xt.tile([P, PACK, P], F32)
                for j in range(PACK):
                    words = x_of[c][:, j, g * GROUP : (g + 1) * GROUP].bitcast(F32)
                    nc.tensor.transpose(xt[:, j, :], words, ident_f32[:])
                xt_of[q] = xt[:].rearrange("w j p -> w (j p)").bitcast(BF16).rearrange("w (q e) -> w e q", e=PAIR)

        def inverse_norm(c):
            rn = small.tile([P, chunks[c][2] // P], F32)
            nc.scalar.activation(out=rn[:], in_=ss_of[c][:], func=ACT.Abs_reciprocal_sqrt, bias=EPS)
            rn_of[c] = rn

        def square_step(s):
            q, e = steps[s]
            c, g = blocks[q]
            if g == 0 and e == 0:
                ss = small.tile([P, chunks[c][2] // P], F32)
                ss_of[c] = ss
            i = PAIR * g + e
            junk = junk_pool.tile([P, CHANNELS], BF16, tag="junk")
            nc.scalar.activation(
                out=junk[:], in_=xt_of[q][:, e, :], func=ACT.Square, accum_out=ss_of[c][:, i : i + 1]
            )
            late = blocks[steps[s - 1][0]][0] if s > 0 else 0
            if late >= 4 and s - 1 == last_step[late]:
                inverse_norm(late)
            if s == last_step[c] and (c < 4 or c == n_chunks - 1):
                inverse_norm(c)
            if e == 0 and q + 2 < len(blocks):
                transpose_block(q + 2)

        def spread(c):
            tiles = chunks[c][2] // P
            pair = min(tiles, PAIR)
            bc = ps_bc.tile([P, pair, tiles // pair * P], F32)
            for i in range(tiles):
                g, e = divmod(i, pair)
                nc.tensor.transpose(
                    bc[:, e, g * P : (g + 1) * P], rn_of[c][:, i : i + 1].to_broadcast([P, P]), ident_f32[:]
                )
            bc_of[c] = bc[:].rearrange("p e w -> p w e")

        def copy_factors_for_gpsimd(c):
            b, w0, pixels, vec = chunks[c]
            bc_tail = small.tile([P, (pixels - vec) // PAIR, PAIR], F32)
            nc.scalar.copy(out=bc_tail[:], in_=bc_of[c][:, vec // PAIR : pixels // PAIR, :])
            bc_tail_of[c] = bc_tail

        def normalise_on_gpsimd(c):
            b, w0, pixels, vec = chunks[c]
            nc.gpsimd.tensor_tensor(
                out=grouped_of[c][:, vec:pixels, :],
                in0=x_of[c][:, :, vec:pixels].rearrange("p j w -> p w j"),
                in1=bc_tail_of[c][:]
                .rearrange("p w e -> p (w e)")
                .unsqueeze(2)
                .to_broadcast([P, pixels - vec, PACK]),
                op=ALU.mult,
            )

        def normalise_on_vector(c):
            b, w0, pixels, vec = chunks[c]
            pair = min(pixels // P, PAIR)
            nc.vector.tensor_tensor(
                out=grouped_of[c][:, 0:vec, :].rearrange("p (w e) j -> p w e j", e=pair),
                in0=x_of[c][:, :, 0:vec].rearrange("p j (w e) -> p w e j", e=pair),
                in1=bc_of[c][:, 0 : vec // pair, :].unsqueeze(3).to_broadcast([P, vec // pair, pair, PACK]),
                op=ALU.mult,
            )

        def quantise_and_multiply(c):
            tiles = chunks[c][2] // P
            codes = work.tile([P, tiles * P], U32, align_bytes=64)
            scales = work.tile([P, tiles * P], U8, align_bytes=64)
            nc.vector.quantize_mx(
                out=codes[:].bitcast(FP8X4),
                scales=scales[:],
                in_=grouped_of[c][:].rearrange("p w j -> p (w j)"),
            )
            sim = ps_sim.tile([P, tiles, PROTOS], F32)
            for i in range(tiles):
                cols = slice(i * P, (i + 1) * P)
                nc.tensor.matmul_mx(
                    out=sim[:, i, :],
                    lhsT=codes[:, cols].bitcast(FP8X4),
                    lhsT_scale=scales[:, cols],
                    rhs=pro_codes[:].bitcast(FP8X4),
                    rhs_scale=pro_scales[:],
                    start=True,
                    stop=True,
                )
            sim_of[c] = sim

        def reduce_over_prototypes(c, op, into):
            b, w0, pixels, vec = chunks[c]
            t0 = w0 // P
            nc.vector.tensor_reduce(
                out=into[:, b, :, t0 : t0 + pixels // P].rearrange("m n i -> m i n"),
                in_=sim_of[c][:].rearrange("m i (n k) -> m i n k", k=PER_CLASS),
                axis=AXIS_X,
                op=op,
            )

        def sum_on_scalar(c):
            b, w0, pixels, vec = chunks[c]
            for i in range(pixels // P):
                for n in range(CLASSES):
                    t = w0 // P + i
                    summed = junk_pool.tile([P, PER_CLASS], F32, tag="summed")
                    nc.scalar.activation(
                        out=summed[:],
                        in_=sim_of[c][:, i, n * PER_CLASS : (n + 1) * PER_CLASS],
                        func=ACT.Copy,
                        accum_out=total[:, b, n, t : t + 1],
                    )

        pro_ss = small.tile([P, 1], F32)
        pro_junk = junk_pool.tile([P, CHANNELS], BF16, tag="junk")
        nc.scalar.activation(out=pro_junk[:], in_=pro_raw[:], func=ACT.Square, accum_out=pro_ss[:])
        pro_rn = small.tile([P, 1], F32)
        nc.scalar.activation(out=pro_rn[:], in_=pro_ss[:], func=ACT.Abs_reciprocal_sqrt, bias=EPS)

        gram = ps_sim.tile([P, P], F32, tag="sim")
        for j in range(PACK):
            nc.tensor.matmul(
                gram[:], lhsT=x_of[0][:, j, :], rhs=x_of[0][:, j, :], start=(j == 0), stop=(j == PACK - 1)
            )
        diagonal = keep.tile([P, P], F32)
        ss = small.tile([P, 1], F32)
        nc.vector.scalar_tensor_tensor(
            out=diagonal[:],
            in0=gram[:],
            scalar=1.0,
            in1=ident_f32[:],
            op0=ALU.mult,
            op1=ALU.mult,
            accum_out=ss[:],
        )
        ss_of[0] = ss
        inverse_norm(0)
        pro_unit = keep.tile([P, CHANNELS], BF16)
        nc.vector.tensor_scalar(
            out=pro_unit[:],
            in0=pro_raw[:],
            scalar1=pro_rn[:, 0:1],
            scalar2=None,
            op0=ALU.mult,
        )
        transpose_block(0)
        spread(0)
        transpose_block(1)
        pro_words = pro_unit[:].bitcast(F32)
        pro_t = ps_misc.tile([P, PAIR, P], F32, tag="misc")
        for u in range(PAIR):
            nc.tensor.transpose(pro_t[:, u, :], pro_words[:, u : CHANNELS // PAIR : PAIR], ident_f32[:])
        next_step = 0

        pro_grouped = keep.tile([P, P, PACK], BF16, align_bytes=64)
        pro_codes = keep.tile([P, PROTOS], U32, align_bytes=64)
        pro_scales = keep.tile([P, PROTOS], U8, align_bytes=64)

        for r in range(n_chunks):
            if r + 1 < n_chunks:
                while next_step <= min(last_step[r + 1] + (1 if r + 1 >= 4 else 0), len(steps) - 1):
                    square_step(next_step)
                    next_step += 1
                spread(r + 1)
                if next_step < len(steps):
                    square_step(next_step)
                    next_step += 1
                if chunks[r + 1][3] < chunks[r + 1][2]:
                    copy_factors_for_gpsimd(r + 1)
            grouped = group_pool.tile([P, chunks[r][2], PACK], BF16, align_bytes=64)
            grouped_of[r] = grouped
            if chunks[r][3] < chunks[r][2]:
                normalise_on_gpsimd(r)
            normalise_on_vector(r)
            if r == 0:
                nc.vector.tensor_copy(
                    out=pro_grouped[:].rearrange("p m t -> p (m t)").bitcast(F32),
                    in_=pro_t[:].rearrange("p u m -> p m u"),
                )
                nc.vector.quantize_mx(
                    out=pro_codes[:].bitcast(FP8X4),
                    scales=pro_scales[:],
                    in_=pro_grouped[:].rearrange("p m t -> p (m t)"),
                )
            else:
                reduce_over_prototypes(r - 1, ALU.max, best)
                if r - 1 in SCALAR_SUMS:
                    sum_on_scalar(r - 1)
            quantise_and_multiply(r)
            if r > 0 and r - 1 not in SCALAR_SUMS:
                reduce_over_prototypes(r - 1, ALU.add, total)
        reduce_over_prototypes(n_chunks - 1, ALU.max, best)
        reduce_over_prototypes(n_chunks - 1, ALU.add, total)

        warm2 = const.tile([P, 1], F32)
        nc.scalar.activation(out=warm2[:], in_=rn_of[n_chunks - 1][:, 0:1], func=ACT.Sigmoid)

        half = BATCH * CLASSES * TILES_PER_IMAGE
        both = keep.tile([P, 2, half], F32)
        nc.vector.scalar_tensor_tensor(
            out=both[:],
            in0=total[:].rearrange("m b n t -> m (b n t)").unsqueeze(1).to_broadcast([P, 2, half]),
            scalar=1.0 / PER_CLASS,
            in1=best[:].rearrange("m b n t -> m (b n t)").unsqueeze(1).to_broadcast([P, 2, half]),
            op0=ALU.mult,
            op1=ALU.add,
        )
        for_vector = ps_misc.tile([P, P], F32, tag="misc")
        nc.tensor.transpose(for_vector[:], both[:].rearrange("m o c -> m (o c)"), ident_f32[:])
        for_scalar = ps_bc.tile([P, P], F32, tag="bc")
        nc.tensor.transpose(for_scalar[:], both[:].rearrange("m o c -> m (o c)"), ident_f32[:])
        result = keep.tile([P, P], F32)
        nc.vector.tensor_scalar(
            out=result[0:half, :], in0=for_vector[0:half, :], scalar1=0.5, scalar2=None, op0=ALU.mult
        )
        nc.scalar.activation(out=result[half:P, :], in_=for_scalar[half:P, :], func=ACT.Sigmoid, scale=0.5)
        nc.sync.dma_start(
            out=out_1.rearrange("b n (t r) w -> (b n t) (r w)", t=TILES_PER_IMAGE), in_=result[0:half, :]
        )
        nc.scalar.dma_start(
            out=out_0.rearrange("b n (t r) w -> (b n t) (r w)", t=TILES_PER_IMAGE), in_=result[half:P, :]
        )
